import numpy as np
import ml_dtypes


BF16 = ml_dtypes.bfloat16


def bf(x):
    return np.asarray(x, np.float32).astype(BF16)


def f64(x):
    return np.asarray(x).astype(np.float64)


E2M1 = np.array([0.0, 0.5, 1.0, 1.5, 2.0, 3.0, 4.0, 6.0, -0.0, -0.5, -1.0, -1.5, -2.0, -3.0, -4.0, -6.0])


def pack_weight(w, fmt):
    k, n = w.shape
    w = f64(bf(w)).reshape(k // 32, 32, n)
    amax = np.abs(w).max(1)
    if fmt == "e4m3":
        byte = np.frexp(amax)[1] - 1 + 127 - 7
    else:
        mant, ex = np.frexp(amax / 6.0)
        byte = np.where(mant > 0.5, ex, ex - 1) + 127
    byte = np.clip(np.where(amax > 0, byte, 1), 1, 254)
    scaled = (w * np.exp2(127.0 - byte)[:, None, :]).reshape(k, n).astype(np.float32)
    by_word = np.ascontiguousarray(scaled.reshape(k // 512, 128, 4, n).transpose(0, 1, 3, 2))
    if fmt == "e4m3":
        words = by_word.astype(ml_dtypes.float8_e4m3fn).view(np.uint8)
    else:
        c = by_word.astype(ml_dtypes.float4_e2m1fn).view(np.uint8) & 0xF
        words = c[..., 0::2] | (c[..., 1::2] << 4)
    return np.ascontiguousarray(words), np.ascontiguousarray(byte.astype(np.uint8).reshape(k // 512, 16, n))


def unpack_weight(words, scales, fmt):
    g, p, n, _ = words.shape
    if fmt == "e4m3":
        vals = np.ascontiguousarray(words).view(ml_dtypes.float8_e4m3fn).astype(np.float64)
    else:
        nib = np.empty((g, p, n, 4), np.uint8)
        nib[..., 0::2] = words & 0xF
        nib[..., 1::2] = words >> 4
        vals = E2M1[nib]
    vals = vals * np.repeat(np.exp2(scales.astype(np.float64) - 127.0), 8, axis=1)[..., None]
    return vals.transpose(0, 1, 3, 2).reshape(g * 512, n)

def pack4(w):
    words, scales = pack_weight(w, "e2m1")
    return words.reshape(words.shape[0], 128, -1), scales


def unpack4(words, scales):
    return unpack_weight(words.reshape(words.shape[0], 128, -1, 2), scales, "e2m1")


def kspread(k):
    return np.exp2(np.repeat(np.random.randint(-6, 7, k // 32), 32).astype(np.float64))


B, S, DIM, HEADS, L, WIN, DIL = 1, 128, 4096, 8, 128, 4, 2
HD = DIM // HEADS
HALF = HD // 2
EPS = 1e-6


def rms_norm(u, g):
    var = np.mean(u * u, axis=-1, keepdims=True)
    return u * (1.0 / np.sqrt(var + EPS)) * g


def rope_apply(u, theta):
    b, s, c = u.shape
    ur = u.reshape(b, s, HEADS, HALF, 2)
    cos = np.cos(theta)[None]
    sin = np.sin(theta)[None]
    u0, u1 = ur[..., 0], ur[..., 1]
    o0 = u0 * cos - u1 * sin
    o1 = u0 * sin + u1 * cos
    return np.stack([o0, o1], axis=-1).reshape(b, s, c)


def setup_inputs():
    s = kspread(DIM)
    sc = 1.0 / np.sqrt(DIM)
    r = np.random.standard_normal
    x = r((B, S, DIM)) * s
    x_words, x_scales = pack4(x.reshape(B * S, DIM).T)
    freqs = bf(np.random.uniform(0.0, 2.0 * np.pi, (S, 1, HALF)))
    Wq_words, Wq_scales = pack4(r((DIM, DIM)) * sc / s[:, None])
    bq = bf(r(DIM) * 0.3)
    Wk_words, Wk_scales = pack4(r((DIM, DIM)) * sc / s[:, None])
    bk = bf(r(DIM) * 0.3)
    gq = bf(1.5 * (1.0 + 0.1 * r(DIM)))
    gk = bf(1.5 * (1.0 + 0.1 * r(DIM)))
    return {"x_words": x_words, "x_scales": x_scales,
            "freqs": freqs,
            "Wq_words": Wq_words, "Wq_scales": Wq_scales, "bq": bq,
            "Wk_words": Wk_words, "Wk_scales": Wk_scales, "bk": bk,
            "gq": gq, "gk": gk}


def reference(x_words, x_scales, freqs, Wq_words, Wq_scales, bq, Wk_words, Wk_scales, bk, gq, gk):
    xq = unpack4(x_words, x_scales).T.reshape(B, S, DIM)
    q = rms_norm((xq @ unpack4(Wq_words, Wq_scales)) + f64(bq), f64(gq))
    k = rms_norm((xq @ unpack4(Wk_words, Wk_scales)) + f64(bk), f64(gk))
    th = f64(freqs)
    return rope_apply(q, th), rope_apply(k, th)

@@ -1,0 +1,320 @@
+from contextlib import ExitStack
+import math
+
+import concourse.mybir as mybir
+from concourse.masks import make_identity
+
+FLOPS = 2 * 128 * 4096 * 8192
+
+F32 = mybir.dt.float32
+BF16 = mybir.dt.bfloat16
+U8 = mybir.dt.uint8
+I32 = mybir.dt.int32
+FP4X4 = mybir.dt.float4_e2m1fn_x4
+ALU = mybir.AluOpType
+ACT = mybir.ActivationFunctionType
+AX = mybir.AxisListType
+
+P = 128
+DIM = 4096
+GROUPS = 8
+TILE_N = 512
+HALF = 256
+STRETCH = 2048
+EPS = 1e-6
+LOOKAHEAD = 4
+
+CHUNKS = (
+    (0, 0, 2048, (2, 2, 2, 2)),
+    (0, 2048, 2048, (2, 2, 2, 2)),
+    (1, 0, 2048, (2, 2, 2, 2)),
+    (1, 2048, 1024, (4, 4)),
+    (1, 3072, 512, (8,)),
+    (1, 3584, 512, (4, 2, 2)),
+)
+LAST_CHUNK = (1, 5)
+
+HEAD_TABLES = ((0, 0), (1, 0), (0, 1), (1, 1))
+TABLE_PLAN = (
+    ((0, 2), (1, 2)),
+    ((0, 3), (1, 3)),
+    ((2, 0), (3, 0)),
+    ((2, 1), (3, 1)),
+    ((2, 2), (3, 2)),
+    ((2, 3), (3, 3)),
+)
+
+
+def tile_selfattention_pa_kernel(
+    tc, x_words, x_scales, freqs, Wq_words, Wq_scales, bq, Wk_words, Wk_scales, bk, gq, gk, out_0, out_1
+):
+    nc = tc.nc
+    w_words = (Wq_words, Wk_words)
+    w_scales = (Wq_scales, Wk_scales)
+    outs = (out_0.rearrange("b s d -> (b s) d"), out_1.rearrange("b s d -> (b s) d"))
+
+    pieces = []
+    for ci, chunk in enumerate(CHUNKS):
+        g0 = 0
+        for gp in chunk[3]:
+            pieces.append((ci, g0, gp))
+            g0 += gp
+
+    with ExitStack() as ctx:
+        const = ctx.enter_context(tc.tile_pool(name="const", bufs=1))
+        codes = ctx.enter_context(tc.tile_pool(name="codes", bufs=7))
+        work = ctx.enter_context(tc.tile_pool(name="work", bufs=2))
+        pcos = ctx.enter_context(tc.psum_pool(name="pcos", bufs=1))
+        psum = ctx.enter_context(tc.psum_pool(name="psum", bufs=7))
+        ctx.enter_context(tc.manual_schedule())
+
+        rows = const.tile([P, TILE_N], BF16, name="rows", tag="rows")
+        warm = const.tile([P, 2], F32, name="warm", tag="warm")
+        eps_t = const.tile([P, 1], F32, name="eps_t", tag="eps_t")
+        xw = const.tile([P, GROUPS, 256], U8, name="xw", tag="xw", align_bytes=64)
+        xs = const.tile([P, GROUPS, P], U8, name="xs", tag="xs", align_bytes=64)
+        planes = const.tile([P, 2, GROUPS, STRETCH], U8, name="planes", tag="planes", align_bytes=64)
+        fr = const.tile([P, HALF], BF16, name="fr", tag="fr")
+        ident = const.tile([P, P], BF16, name="ident", tag="ident")
+        identf = const.tile([P, P], F32, name="identf", tag="identf")
+        tabs = []
+        for v in range(4):
+            tab = const.tile([P, DIM], BF16, name="tab%d" % v, tag="tab%d" % v)
+            tabs.append(tab)
+        res = []
+        for tn in range(2):
+            o = const.tile([P, DIM], F32, name="res%d" % tn, tag="res%d" % tn)
+            res.append(o)
+        ss = const.tile([P, 32], F32, name="ss", tag="ss")
+        cos_sb = const.tile([P, TILE_N], F32, name="cos_sb", tag="cos_sb")
+        sin2 = const.tile([P, 2 * TILE_N], F32, name="sin2", tag="sin2")
+        cos2 = pcos.tile([P, TILE_N], F32, name="cos2", tag="cos2")
+
+        for v, vec in enumerate((bq, gq, bk, gk)):
+            nc.scalar.dma_start(out=rows[8 * v : 8 * v + 8, :], in_=vec.rearrange("(s n) -> s n", n=TILE_N))
+        nc.scalar.dma_start(out=fr[:], in_=freqs.rearrange("s o j -> s (o j)"))
+
+        nc.vector.memset(warm[:], 0.0)
+        nc.vector.memset(rows[32:64, :], 0.0)
+        nc.vector.memset(rows[64:128, :], 0.0)
+        nc.vector.memset(xs[:].bitcast(I32), 0)
+        nc.vector.memset(planes[:, 0].bitcast(I32), 0)
+        nc.vector.memset(eps_t[:], EPS)
+        make_identity(nc, ident[:])
+        for g in range(0, GROUPS, 2):
+            nc.gpsimd.memset(planes[:, 1, g : g + 2].bitcast(F32), 0.0)
+        make_identity(nc, identf[:])
+        nc.scalar.activation(out=warm[:, 1:2], in_=warm[:, 0:1], func=ACT.Sin)
+
+        code_tiles = {}
+        banks = {}
+
+        def load_scales(dst, src):
+            for r in range(4):
+                nc.sync.dma_start(
+                    out=dst[r:P:32].bitcast(I32),
+                    in_=src[:, r:16:4, :].rearrange("g q n -> q g n").bitcast(I32),
+                )
+
+        def plane_of(tn, c0):
+            return planes[:, (2 * tn + c0 // STRETCH) % 2]
+
+        def load_codes(j):
+            ci, g0, gp = pieces[j]
+            tn, c0, n = CHUNKS[ci][0:3]
+            wc = codes.tile([P, gp, 2 * n], U8, name="wc", tag="wc", align_bytes=64)
+            nc.sync.dma_start(
+                out=wc[:].bitcast(I32),
+                in_=w_words[tn][g0 : g0 + gp, :, 2 * c0 : 2 * (c0 + n)].rearrange("g p b -> p g b").bitcast(I32),
+            )
+            code_tiles[j] = wc
+
+        def load_piece(j):
+            ci, g0, gp = pieces[j]
+            tn, c0, n = CHUNKS[ci][0:3]
+            if g0 == 0 and c0 % STRETCH == 0:
+                load_scales(plane_of(tn, c0), w_scales[tn][:, :, c0 : c0 + STRETCH])
+            load_codes(j)
+
+        def spread(v, h):
+            bank = psum.tile([P, 2 * TILE_N], BF16, name="tb", tag="bank")
+            for u in range(2):
+                r = 8 * v + 2 * h + u
+                nc.tensor.matmul(
+                    out=bank[:, TILE_N * u : TILE_N * (u + 1)],
+                    lhsT=ident[:, r : r + 1].to_broadcast([P, P]),
+                    rhs=rows[:],
+                    start=True,
+                    stop=True,
+                )
+            nc.scalar.copy(out=tabs[v][:, 1024 * h : 1024 * (h + 1)], in_=bank[:])
+
+        nc.sync.dma_start(out=xw[:].bitcast(I32), in_=x_words.rearrange("g p b -> p g b").bitcast(I32))
+        load_codes(0)
+        load_scales(xs, x_scales)
+        load_scales(plane_of(0, 0), w_scales[0][:, :, 0:STRETCH])
+        for j in range(1, LOOKAHEAD):
+            load_codes(j)
+
+        for v, h in HEAD_TABLES[0:4]:
+            spread(v, h)
+
+        two_pi = 2.0 * math.pi
+        c_hi = 6.28125
+        c_lo = two_pi - c_hi
+        ki = const.tile([P, HALF], I32, name="ki", tag="ki")
+        kf = const.tile([P, HALF], F32, name="kf", tag="kf")
+        ra = const.tile([P, HALF], F32, name="ra", tag="ra")
+        rb = const.tile([P, HALF], F32, name="rb", tag="rb")
+        ma = const.tile([P, HALF], F32, name="ma", tag="ma")
+        mb = const.tile([P, HALF], F32, name="mb", tag="mb")
+        rd = const.tile([P, HALF], F32, name="rd", tag="rd")
+        ab = const.tile([P, HALF], F32, name="ab", tag="ab")
+        pm = const.tile([P, 2, HALF], F32, name="pm", tag="pm")
+        cc = const.tile([P, 2, HALF], F32, name="cc", tag="cc")
+        nc.vector.tensor_scalar(out=ki[:], in0=fr[:], scalar1=1.0 / two_pi, scalar2=None, op0=ALU.mult)
+        nc.vector.tensor_copy(out=kf[:], in_=ki[:])
+        nc.vector.scalar_tensor_tensor(out=ra[:], in0=kf[:], scalar=-c_hi, in1=fr[:], op0=ALU.mult, op1=ALU.add)
+        nc.vector.scalar_tensor_tensor(out=rb[:], in0=kf[:], scalar=-c_lo, in1=ra[:], op0=ALU.mult, op1=ALU.add)
+        nc.vector.tensor_scalar(out=ma[:], in0=rb[:], scalar1=math.pi, scalar2=-two_pi, op0=ALU.is_gt, op1=ALU.mult)
+        nc.vector.tensor_scalar(out=mb[:], in0=rb[:], scalar1=-math.pi, scalar2=two_pi, op0=ALU.is_lt, op1=ALU.mult)
+        nc.vector.tensor_tensor(out=ra[:], in0=rb[:], in1=ma[:], op=ALU.add)
+        nc.vector.tensor_tensor(out=rd[:], in0=ra[:], in1=mb[:], op=ALU.add)
+        nc.vector.scalar_tensor_tensor(out=ma[:], in0=rd[:], scalar=-1.0, in1=rd[:], op0=ALU.mult, op1=ALU.min)
+        nc.vector.tensor_scalar(out=ab[:], in0=ma[:], scalar1=0.5 * math.pi, scalar2=None, op0=ALU.add)
+        nc.scalar.activation(out=pm[:, 0, :], in_=rd[:], func=ACT.Sin, scale=-1.0)
+        nc.scalar.activation(out=pm[:, 1, :], in_=rd[:], func=ACT.Sin)
+        nc.scalar.activation(out=cc[:, 0, :], in_=ab[:], func=ACT.Sin)
+        nc.scalar.activation(out=cc[:, 1, :], in_=ab[:], func=ACT.Sin)
+        nc.vector.tensor_copy(out=cos_sb[:].rearrange("p (j e) -> p j e", e=2), in_=cc[:].rearrange("p e j -> p j e"))
+        for dup in range(2):
+            nc.vector.tensor_copy(
+                out=sin2[:, TILE_N * dup : TILE_N * (dup + 1)].rearrange("p (j e) -> p j e", e=2),
+                in_=pm[:].rearrange("p e j -> p j e"),
+            )
+
+
+        def run_passes(i):
+            ci, g0, gp = pieces[i]
+            tn, c0, n = CHUNKS[ci][0:3]
+            if g0 == 0:
+                accs = []
+                for ti in range(n // TILE_N):
+                    acc = psum.tile([P, TILE_N], F32, name="acc", tag="bank")
+                    accs.append(acc)
+                banks[ci] = accs
+            plane = plane_of(tn, c0)
+            pc = c0 % STRETCH
+            wc = code_tiles[i]
+            for gi in range(gp):
+                g = g0 + gi
+                for ti, acc in enumerate(banks[ci]):
+                    nc.tensor.matmul_mx(
+                        out=acc[:],
+                        lhsT=xw[:, g, :].bitcast(FP4X4),
+                        lhsT_scale=xs[:, g, :],
+                        rhs=wc[:, gi, 2 * TILE_N * ti : 2 * TILE_N * (ti + 1)].bitcast(FP4X4),
+                        rhs_scale=plane[:, g, pc + TILE_N * ti : pc + TILE_N * (ti + 1)],
+                        start=(g == 0),
+                        stop=(g == GROUPS - 1),
+                    )
+
+        ss_next = [0, 16]
+
+        def swapped(ap):
+            return ap.rearrange("p (j e) -> p j e", e=2)[:, :, ::-1]
+
+        def paired(ap):
+            return ap.rearrange("p (j e) -> p j e", e=2)
+
+        def scale_on_scalar(tn, rs, lo, hi):
+            nc.scalar.activation(out=res[tn][:, lo:hi], in_=res[tn][:, lo:hi], func=ACT.Copy, scale=rs[:])
+
+        def epilogue(ci):
+            tn, c0, n = CHUNKS[ci][0:3]
+            uw = n // 2
+            sub = min(uw, TILE_N)
+            o = res[tn]
+            closing = ci in LAST_CHUNK
+            cols = (c0, c0 + uw)
+            t_of = {}
+            w_of = {}
+            s_of = {}
+            for col in cols:
+                t = work.tile([P, 2 * TILE_N], F32, name="t", tag="t", bufs=4)
+                for k0 in range(0, uw, sub):
+                    rel = col + k0 - c0
+                    acc = banks[ci][rel // TILE_N]
+                    nc.vector.tensor_tensor(
+                        out=t[:, k0 : k0 + sub],
+                        in0=acc[:, rel % TILE_N : rel % TILE_N + sub],
+                        in1=tabs[2 * tn][:, col + k0 : col + k0 + sub],
+                        op=ALU.add,
+                    )
+                junk = work.tile([P, 2 * TILE_N], F32, name="junk", tag="junk", bufs=1)
+                nc.scalar.activation(
+                    out=junk[:, 0:uw],
+                    in_=t[:, 0:uw],
+                    func=ACT.Square,
+                    scale=1.0 / 64.0,
+                    accum_out=ss[:, ss_next[tn] : ss_next[tn] + 1],
+                )
+                ss_next[tn] += 1
+                t_of[col] = t
+            for col in cols:
+                w = work.tile([P, 2 * TILE_N], F32, name="w", tag="w", bufs=4)
+                nc.vector.tensor_tensor(
+                    out=w[:, 0:uw], in0=t_of[col][:, 0:uw], in1=tabs[2 * tn + 1][:, col : col + uw], op=ALU.mult
+                )
+                w_of[col] = w
+                a = col % TILE_N
+                s = work.tile([P, 2 * TILE_N], F32, name="s", tag="s", bufs=3)
+                nc.gpsimd.tensor_tensor(
+                    out=paired(s[:, 0:uw]), in0=swapped(w[:, 0:uw]), in1=paired(sin2[:, a : a + uw]), op=ALU.mult
+                )
+                s_of[col] = s
+            if closing:
+                ms = const.tile([P, 1], F32, name="ms%d" % tn, tag="ms%d" % tn)
+                sd = const.tile([P, 1], F32, name="sd%d" % tn, tag="sd%d" % tn)
+                rs = const.tile([P, 1], F32, name="rs%d" % tn, tag="rs%d" % tn)
+                nc.vector.tensor_reduce(out=ms[:], in_=ss[:, 16 * tn : ss_next[tn]], axis=AX.X, op=ALU.add)
+                nc.scalar.activation(out=sd[:], in_=ms[:], func=ACT.Sqrt, bias=eps_t[:], scale=1.0)
+            for col in cols:
+                for k0 in range(0, uw, sub):
+                    a = (col + k0) % TILE_N
+                    nc.vector.tensor_tensor(
+                        out=o[:, col + k0 : col + k0 + sub], in0=w_of[col][:, k0 : k0 + sub], in1=cos2[:, a : a + sub], op=ALU.mult
+                    )
+                nc.gpsimd.tensor_tensor(
+                    out=o[:, col : col + uw], in0=o[:, col : col + uw], in1=s_of[col][:, 0:uw], op=ALU.add
+                )
+            if closing:
+                nc.vector.reciprocal(out=rs[:], in_=sd[:])
+                for lo in range(0, c0, 1024):
+                    scale_on_scalar(tn, rs, lo, min(lo + 1024, c0))
+                if uw >= TILE_N:
+                    for col in cols:
+                        scale_on_scalar(tn, rs, col, col + uw)
+                else:
+                    scale_on_scalar(tn, rs, c0, c0 + n)
+
+        def store(tn, blk):
+            nc.sync.dma_start(out=outs[tn][:, 1024 * blk : 1024 * (blk + 1)], in_=res[tn][:, 1024 * blk : 1024 * (blk + 1)])
+
+        for i in range(len(pieces)):
+            if i + LOOKAHEAD < len(pieces):
+                load_piece(i + LOOKAHEAD)
+            if i + LOOKAHEAD == len(pieces):
+                for blk in range(4):
+                    store(0, blk)
+            if i < len(TABLE_PLAN):
+                for v, h in TABLE_PLAN[i]:
+                    spread(v, h)
+            if i == 2:
+                nc.tensor.matmul(out=cos2[:], lhsT=identf[:], rhs=cos_sb[:], start=True, stop=True)
+            run_passes(i)
+            ci, g0, gp = pieces[i]
+            if g0 + gp == GROUPS:
+                epilogue(ci)
+        for blk in range(4):
+            store(1, blk)

@@ -110,10 +110,10 @@ def tile_selfattention_pa_kernel(
         banks = {}
 
         def load_scales(dst, src):
-            for r in range(4):
+            for quad in (0, 2, 1, 3):
                 nc.sync.dma_start(
-                    out=dst[r:P:32].bitcast(I32),
-                    in_=src[:, r:16:4, :].rearrange("g q n -> q g n").bitcast(I32),
+                    out=dst[32 * quad : 32 * quad + 4].bitcast(I32),
+                    in_=src[:, 4 * quad : 4 * quad + 4, :].rearrange("g r n -> r g n").bitcast(I32),
                 )
 
         def plane_of(tn, c0):

@@ -21,28 +21,54 @@ GROUPS = 8
 TILE_N = 512
 HALF = 256
 STRETCH = 2048
+SETS = 3
 EPS = 1e-6
 LOOKAHEAD = 4
 
 CHUNKS = (
-    (0, 0, 2048, (2, 2, 2, 2)),
-    (0, 2048, 2048, (2, 2, 2, 2)),
-    (1, 0, 2048, (2, 2, 2, 2)),
+    (0, 0, 1024, (4, 4)),
+    (0, 1024, 1024, (4, 4)),
+    (0, 2048, 1024, (4, 4)),
+    (0, 3072, 1024, (4, 4)),
+    (1, 0, 1024, (4, 4)),
+    (1, 1024, 1024, (4, 4)),
     (1, 2048, 1024, (4, 4)),
     (1, 3072, 512, (8,)),
     (1, 3584, 512, (4, 2, 2)),
 )
-LAST_CHUNK = (1, 5)
+LAST_CHUNK = (3, 8)
 
-HEAD_TABLES = ((0, 0), (1, 0), (0, 1), (1, 1))
+BEFORE = {
+    1: ((0, 1),),
+    2: ((0, 2), (1, 0)),
+    3: ((0, 3), (1, 1)),
+    4: ((1, 2), (2, 0)),
+    5: ((1, 3), (2, 1)),
+    6: ((2, 2),),
+    7: ((2, 3),),
+    9: ((3, 0),),
+    10: ((3, 1),),
+    11: ((3, 2),),
+    12: ((3, 3),),
+}
+STORE_AFTER = {17: (0, 1, 2, 3)}
+
+HEAD_TABLES = ((3, 0), (3, 1), (3, 2), (3, 3), (0, 0), (1, 0))
 TABLE_PLAN = (
+    ((0, 1), (1, 1)),
     ((0, 2), (1, 2)),
     ((0, 3), (1, 3)),
-    ((2, 0), (3, 0)),
-    ((2, 1), (3, 1)),
-    ((2, 2), (3, 2)),
-    ((2, 3), (3, 3)),
+    ((2, 0), (2, 1)),
+    ((2, 2), (2, 3)),
 )
+
+
+def swapped(ap):
+    return ap.rearrange("p (j e) -> p j e", e=2)[:, :, ::-1]
+
+
+def paired(ap):
+    return ap.rearrange("p (j e) -> p j e", e=2)
 
 
 def tile_selfattention_pa_kernel(
@@ -60,12 +86,26 @@ def tile_selfattention_pa_kernel(
             pieces.append((ci, g0, gp))
             g0 += gp
 
+    first_piece = {}
+    last_piece = {}
+    for j, piece in enumerate(pieces):
+        st = 2 * CHUNKS[piece[0]][0] + CHUNKS[piece[0]][1] // STRETCH
+        first_piece.setdefault(st, j)
+        last_piece[st] = j
+    emit_after = {}
+    floor = -1
+    for j in range(len(pieces)):
+        floor = max(floor, j - LOOKAHEAD)
+        for st, r in BEFORE.get(j, ()):
+            if st >= SETS:
+                floor = max(floor, last_piece[st - SETS])
+            assert floor < first_piece[st]
+        emit_after[j] = floor
+
     with ExitStack() as ctx:
         const = ctx.enter_context(tc.tile_pool(name="const", bufs=1))
-        codes = ctx.enter_context(tc.tile_pool(name="codes", bufs=7))
-        work = ctx.enter_context(tc.tile_pool(name="work", bufs=2))
-        pcos = ctx.enter_context(tc.psum_pool(name="pcos", bufs=1))
-        psum = ctx.enter_context(tc.psum_pool(name="psum", bufs=7))
+        codes = ctx.enter_context(tc.tile_pool(name="codes", bufs=6))
+        psum = ctx.enter_context(tc.psum_pool(name="psum", bufs=8))
         ctx.enter_context(tc.manual_schedule())
 
         rows = const.tile([P, TILE_N], BF16, name="rows", tag="rows")
@@ -73,12 +113,14 @@ def tile_selfattention_pa_kernel(
         eps_t = const.tile([P, 1], F32, name="eps_t", tag="eps_t")
         xw = const.tile([P, GROUPS, 256], U8, name="xw", tag="xw", align_bytes=64)
         xs = const.tile([P, GROUPS, P], U8, name="xs", tag="xs", align_bytes=64)
-        planes = const.tile([P, 2, GROUPS, STRETCH], U8, name="planes", tag="planes", align_bytes=64)
+        planes = []
+        for a in range(SETS):
+            pl = const.tile([P, GROUPS, STRETCH], U8, name="pl%d" % a, tag="pl%d" % a, align_bytes=64)
+            planes.append(pl)
         fr = const.tile([P, HALF], BF16, name="fr", tag="fr")
         ident = const.tile([P, P], BF16, name="ident", tag="ident")
-        identf = const.tile([P, P], F32, name="identf", tag="identf")
         tabs = []
-        for v in range(4):
+        for v in range(3):
             tab = const.tile([P, DIM], BF16, name="tab%d" % v, tag="tab%d" % v)
             tabs.append(tab)
         res = []
@@ -86,40 +128,40 @@ def tile_selfattention_pa_kernel(
             o = const.tile([P, DIM], F32, name="res%d" % tn, tag="res%d" % tn)
             res.append(o)
         ss = const.tile([P, 32], F32, name="ss", tag="ss")
-        cos_sb = const.tile([P, TILE_N], F32, name="cos_sb", tag="cos_sb")
-        sin2 = const.tile([P, 2 * TILE_N], F32, name="sin2", tag="sin2")
-        cos2 = pcos.tile([P, TILE_N], F32, name="cos2", tag="cos2")
+        cos2 = const.tile([P, TILE_N], F32, name="cos2", tag="cos2")
+        sin2 = const.tile([P, TILE_N], F32, name="sin2", tag="sin2")
+        gcos = const.tile([P, DIM], F32, name="gcos", tag="gcos")
+        gsin = const.tile([P, DIM], F32, name="gsin", tag="gsin")
 
         for v, vec in enumerate((bq, gq, bk, gk)):
             nc.scalar.dma_start(out=rows[8 * v : 8 * v + 8, :], in_=vec.rearrange("(s n) -> s n", n=TILE_N))
         nc.scalar.dma_start(out=fr[:], in_=freqs.rearrange("s o j -> s (o j)"))
 
+        nc.vector.memset(planes[0][:].bitcast(I32), 0)
+        nc.vector.memset(xs[:].bitcast(I32), 0)
         nc.vector.memset(warm[:], 0.0)
         nc.vector.memset(rows[32:64, :], 0.0)
         nc.vector.memset(rows[64:128, :], 0.0)
-        nc.vector.memset(xs[:].bitcast(I32), 0)
-        nc.vector.memset(planes[:, 0].bitcast(I32), 0)
         nc.vector.memset(eps_t[:], EPS)
         make_identity(nc, ident[:])
-        for g in range(0, GROUPS, 2):
-            nc.gpsimd.memset(planes[:, 1, g : g + 2].bitcast(F32), 0.0)
-        make_identity(nc, identf[:])
+        for a in range(1, SETS):
+            for g in range(0, GROUPS, 2):
+                nc.gpsimd.memset(planes[a][:, g : g + 2].bitcast(F32), 0.0)
         nc.scalar.activation(out=warm[:, 1:2], in_=warm[:, 0:1], func=ACT.Sin)
 
         code_tiles = {}
         banks = {}
 
-        def load_scales(dst, src):
-            for quad in (0, 2, 1, 3):
-                nc.sync.dma_start(
-                    out=dst[32 * quad : 32 * quad + 4].bitcast(I32),
-                    in_=src[:, 4 * quad : 4 * quad + 4, :].rearrange("g r n -> r g n").bitcast(I32),
-                )
+        def load_scale_row(st, r):
+            src = w_scales[st // 2][:, :, STRETCH * (st % 2) : STRETCH * (st % 2 + 1)]
+            nc.sync.dma_start(
+                out=planes[st % SETS][r:P:32].bitcast(I32),
+                in_=src[:, r:16:4, :].rearrange("g q n -> q g n").bitcast(I32),
+            )
 
-        def plane_of(tn, c0):
-            return planes[:, (2 * tn + c0 // STRETCH) % 2]
-
-        def load_codes(j):
+        def load_piece(j):
+            for st, r in BEFORE.get(j, ()):
+                load_scale_row(st, r)
             ci, g0, gp = pieces[j]
             tn, c0, n = CHUNKS[ci][0:3]
             wc = codes.tile([P, gp, 2 * n], U8, name="wc", tag="wc", align_bytes=64)
@@ -129,14 +171,7 @@ def tile_selfattention_pa_kernel(
             )
             code_tiles[j] = wc
 
-        def load_piece(j):
-            ci, g0, gp = pieces[j]
-            tn, c0, n = CHUNKS[ci][0:3]
-            if g0 == 0 and c0 % STRETCH == 0:
-                load_scales(plane_of(tn, c0), w_scales[tn][:, :, c0 : c0 + STRETCH])
-            load_codes(j)
-
-        def spread(v, h):
+        def spread(v, h, dst):
             bank = psum.tile([P, 2 * TILE_N], BF16, name="tb", tag="bank")
             for u in range(2):
                 r = 8 * v + 2 * h + u
@@ -147,52 +182,66 @@ def tile_selfattention_pa_kernel(
                     start=True,
                     stop=True,
                 )
-            nc.scalar.copy(out=tabs[v][:, 1024 * h : 1024 * (h + 1)], in_=bank[:])
+            nc.scalar.copy(out=dst[:, 1024 * h : 1024 * (h + 1)], in_=bank[:])
 
         nc.sync.dma_start(out=xw[:].bitcast(I32), in_=x_words.rearrange("g p b -> p g b").bitcast(I32))
-        load_codes(0)
-        load_scales(xs, x_scales)
-        load_scales(plane_of(0, 0), w_scales[0][:, :, 0:STRETCH])
-        for j in range(1, LOOKAHEAD):
-            load_codes(j)
-
-        for v, h in HEAD_TABLES[0:4]:
-            spread(v, h)
-
-        two_pi = 2.0 * math.pi
-        c_hi = 6.28125
-        c_lo = two_pi - c_hi
-        ki = const.tile([P, HALF], I32, name="ki", tag="ki")
-        kf = const.tile([P, HALF], F32, name="kf", tag="kf")
-        ra = const.tile([P, HALF], F32, name="ra", tag="ra")
-        rb = const.tile([P, HALF], F32, name="rb", tag="rb")
-        ma = const.tile([P, HALF], F32, name="ma", tag="ma")
-        mb = const.tile([P, HALF], F32, name="mb", tag="mb")
-        rd = const.tile([P, HALF], F32, name="rd", tag="rd")
-        ab = const.tile([P, HALF], F32, name="ab", tag="ab")
-        pm = const.tile([P, 2, HALF], F32, name="pm", tag="pm")
-        cc = const.tile([P, 2, HALF], F32, name="cc", tag="cc")
-        nc.vector.tensor_scalar(out=ki[:], in0=fr[:], scalar1=1.0 / two_pi, scalar2=None, op0=ALU.mult)
-        nc.vector.tensor_copy(out=kf[:], in_=ki[:])
-        nc.vector.scalar_tensor_tensor(out=ra[:], in0=kf[:], scalar=-c_hi, in1=fr[:], op0=ALU.mult, op1=ALU.add)
-        nc.vector.scalar_tensor_tensor(out=rb[:], in0=kf[:], scalar=-c_lo, in1=ra[:], op0=ALU.mult, op1=ALU.add)
-        nc.vector.tensor_scalar(out=ma[:], in0=rb[:], scalar1=math.pi, scalar2=-two_pi, op0=ALU.is_gt, op1=ALU.mult)
-        nc.vector.tensor_scalar(out=mb[:], in0=rb[:], scalar1=-math.pi, scalar2=two_pi, op0=ALU.is_lt, op1=ALU.mult)
-        nc.vector.tensor_tensor(out=ra[:], in0=rb[:], in1=ma[:], op=ALU.add)
-        nc.vector.tensor_tensor(out=rd[:], in0=ra[:], in1=mb[:], op=ALU.add)
-        nc.vector.scalar_tensor_tensor(out=ma[:], in0=rd[:], scalar=-1.0, in1=rd[:], op0=ALU.mult, op1=ALU.min)
-        nc.vector.tensor_scalar(out=ab[:], in0=ma[:], scalar1=0.5 * math.pi, scalar2=None, op0=ALU.add)
-        nc.scalar.activation(out=pm[:, 0, :], in_=rd[:], func=ACT.Sin, scale=-1.0)
-        nc.scalar.activation(out=pm[:, 1, :], in_=rd[:], func=ACT.Sin)
-        nc.scalar.activation(out=cc[:, 0, :], in_=ab[:], func=ACT.Sin)
-        nc.scalar.activation(out=cc[:, 1, :], in_=ab[:], func=ACT.Sin)
-        nc.vector.tensor_copy(out=cos_sb[:].rearrange("p (j e) -> p j e", e=2), in_=cc[:].rearrange("p e j -> p j e"))
-        for dup in range(2):
-            nc.vector.tensor_copy(
-                out=sin2[:, TILE_N * dup : TILE_N * (dup + 1)].rearrange("p (j e) -> p j e", e=2),
-                in_=pm[:].rearrange("p e j -> p j e"),
+        load_scale_row(0, 0)
+        for quad in range(4):
+            nc.sync.dma_start(
+                out=xs[32 * quad : 32 * quad + 4].bitcast(I32),
+                in_=x_scales[:, 4 * quad : 4 * quad + 4, :].rearrange("g r n -> r g n").bitcast(I32),
             )
+        for j in range(len(pieces)):
+            if emit_after[j] < 0:
+                load_piece(j)
 
+        with tc.tile_pool(name="head", bufs=1) as head:
+            gk_tab = head.tile([P, DIM], BF16, name="gk_tab", tag="gk_tab")
+            for v, h in HEAD_TABLES:
+                spread(v, h, gk_tab if v == 3 else tabs[v])
+
+            two_pi = 2.0 * math.pi
+            c_hi = 6.28125
+            c_lo = two_pi - c_hi
+            ki = head.tile([P, HALF], I32, name="ki", tag="ki")
+            kf = head.tile([P, HALF], F32, name="kf", tag="kf")
+            ra = head.tile([P, HALF], F32, name="ra", tag="ra")
+            rb = head.tile([P, HALF], F32, name="rb", tag="rb")
+            ma = head.tile([P, HALF], F32, name="ma", tag="ma")
+            mb = head.tile([P, HALF], F32, name="mb", tag="mb")
+            rd = head.tile([P, HALF], F32, name="rd", tag="rd")
+            ab = head.tile([P, HALF], F32, name="ab", tag="ab")
+            pm = head.tile([P, 2, HALF], F32, name="pm", tag="pm")
+            cc = head.tile([P, 2, HALF], F32, name="cc", tag="cc")
+            nc.vector.tensor_scalar(out=ki[:], in0=fr[:], scalar1=1.0 / two_pi, scalar2=None, op0=ALU.mult)
+            nc.vector.tensor_copy(out=kf[:], in_=ki[:])
+            nc.vector.scalar_tensor_tensor(out=ra[:], in0=kf[:], scalar=-c_hi, in1=fr[:], op0=ALU.mult, op1=ALU.add)
+            nc.vector.scalar_tensor_tensor(out=rb[:], in0=kf[:], scalar=-c_lo, in1=ra[:], op0=ALU.mult, op1=ALU.add)
+            nc.vector.tensor_scalar(out=ma[:], in0=rb[:], scalar1=math.pi, scalar2=-two_pi, op0=ALU.is_gt, op1=ALU.mult)
+            nc.vector.tensor_scalar(out=mb[:], in0=rb[:], scalar1=-math.pi, scalar2=two_pi, op0=ALU.is_lt, op1=ALU.mult)
+            nc.vector.tensor_tensor(out=ra[:], in0=rb[:], in1=ma[:], op=ALU.add)
+            nc.vector.tensor_tensor(out=rd[:], in0=ra[:], in1=mb[:], op=ALU.add)
+            nc.vector.scalar_tensor_tensor(out=ma[:], in0=rd[:], scalar=-1.0, in1=rd[:], op0=ALU.mult, op1=ALU.min)
+            nc.vector.tensor_scalar(out=ab[:], in0=ma[:], scalar1=0.5 * math.pi, scalar2=None, op0=ALU.add)
+            nc.scalar.activation(out=pm[:, 0, :], in_=rd[:], func=ACT.Sin, scale=-1.0)
+            nc.scalar.activation(out=pm[:, 1, :], in_=rd[:], func=ACT.Sin)
+            nc.scalar.activation(out=cc[:, 0, :], in_=ab[:], func=ACT.Sin)
+            nc.scalar.activation(out=cc[:, 1, :], in_=ab[:], func=ACT.Sin)
+            nc.vector.tensor_copy(out=paired(sin2[:]), in_=pm[:].rearrange("p e j -> p j e"))
+            nc.vector.tensor_copy(out=paired(cos2[:]), in_=cc[:].rearrange("p e j -> p j e"))
+
+            for col in range(0, DIM, TILE_N):
+                nc.vector.tensor_tensor(
+                    out=gcos[:, col : col + TILE_N], in0=gk_tab[:, col : col + TILE_N], in1=cos2[:], op=ALU.mult
+                )
+                nc.vector.tensor_tensor(
+                    out=paired(gsin[:, col : col + TILE_N]),
+                    in0=swapped(gk_tab[:, col : col + TILE_N]),
+                    in1=paired(sin2[:]),
+                    op=ALU.mult,
+                )
+
+        work = ctx.enter_context(tc.tile_pool(name="work", bufs=2))
 
         def run_passes(i):
             ci, g0, gp = pieces[i]
@@ -203,7 +252,7 @@ def tile_selfattention_pa_kernel(
                     acc = psum.tile([P, TILE_N], F32, name="acc", tag="bank")
                     accs.append(acc)
                 banks[ci] = accs
-            plane = plane_of(tn, c0)
+            plane = planes[(2 * tn + c0 // STRETCH) % SETS]
             pc = c0 % STRETCH
             wc = code_tiles[i]
             for gi in range(gp):
@@ -221,100 +270,94 @@ def tile_selfattention_pa_kernel(
 
         ss_next = [0, 16]
 
-        def swapped(ap):
-            return ap.rearrange("p (j e) -> p j e", e=2)[:, :, ::-1]
-
-        def paired(ap):
-            return ap.rearrange("p (j e) -> p j e", e=2)
-
         def scale_on_scalar(tn, rs, lo, hi):
             nc.scalar.activation(out=res[tn][:, lo:hi], in_=res[tn][:, lo:hi], func=ACT.Copy, scale=rs[:])
 
         def epilogue(ci):
             tn, c0, n = CHUNKS[ci][0:3]
-            uw = n // 2
-            sub = min(uw, TILE_N)
+            width = min(TILE_N, n // 2)
             o = res[tn]
+            pair = (c0, c0 + width)
             closing = ci in LAST_CHUNK
-            cols = (c0, c0 + uw)
             t_of = {}
             w_of = {}
             s_of = {}
-            for col in cols:
-                t = work.tile([P, 2 * TILE_N], F32, name="t", tag="t", bufs=4)
-                for k0 in range(0, uw, sub):
-                    rel = col + k0 - c0
-                    acc = banks[ci][rel // TILE_N]
-                    nc.vector.tensor_tensor(
-                        out=t[:, k0 : k0 + sub],
-                        in0=acc[:, rel % TILE_N : rel % TILE_N + sub],
-                        in1=tabs[2 * tn][:, col + k0 : col + k0 + sub],
-                        op=ALU.add,
-                    )
-                junk = work.tile([P, 2 * TILE_N], F32, name="junk", tag="junk", bufs=1)
+            for col in pair:
+                acc = banks[ci][(col - c0) // TILE_N]
+                b0 = (col - c0) % TILE_N
+                t = work.tile([P, TILE_N], F32, name="t", tag="t", bufs=6)
+                nc.vector.tensor_tensor(
+                    out=t[:, 0:width], in0=acc[:, b0 : b0 + width], in1=tabs[2 * tn][:, col : col + width], op=ALU.add
+                )
+                junk = work.tile([P, TILE_N], F32, name="junk", tag="junk", bufs=2)
                 nc.scalar.activation(
-                    out=junk[:, 0:uw],
-                    in_=t[:, 0:uw],
+                    out=junk[:, 0:width],
+                    in_=t[:, 0:width],
                     func=ACT.Square,
                     scale=1.0 / 64.0,
                     accum_out=ss[:, ss_next[tn] : ss_next[tn] + 1],
                 )
                 ss_next[tn] += 1
                 t_of[col] = t
-            for col in cols:
-                w = work.tile([P, 2 * TILE_N], F32, name="w", tag="w", bufs=4)
-                nc.vector.tensor_tensor(
-                    out=w[:, 0:uw], in0=t_of[col][:, 0:uw], in1=tabs[2 * tn + 1][:, col : col + uw], op=ALU.mult
-                )
-                w_of[col] = w
+            for col in pair:
+                if tn == 0:
+                    w = work.tile([P, TILE_N], F32, name="w", tag="w", bufs=4)
+                    nc.vector.tensor_tensor(
+                        out=w[:, 0:width], in0=t_of[col][:, 0:width], in1=tabs[1][:, col : col + width], op=ALU.mult
+                    )
+                    w_of[col] = w
+                else:
+                    w_of[col] = t_of[col]
+            for col in pair:
                 a = col % TILE_N
-                s = work.tile([P, 2 * TILE_N], F32, name="s", tag="s", bufs=3)
-                nc.gpsimd.tensor_tensor(
-                    out=paired(s[:, 0:uw]), in0=swapped(w[:, 0:uw]), in1=paired(sin2[:, a : a + uw]), op=ALU.mult
+                nc.vector.tensor_tensor(
+                    out=o[:, col : col + width],
+                    in0=w_of[col][:, 0:width],
+                    in1=cos2[:, a : a + width] if tn == 0 else gcos[:, col : col + width],
+                    op=ALU.mult,
                 )
-                s_of[col] = s
             if closing:
                 ms = const.tile([P, 1], F32, name="ms%d" % tn, tag="ms%d" % tn)
                 sd = const.tile([P, 1], F32, name="sd%d" % tn, tag="sd%d" % tn)
                 rs = const.tile([P, 1], F32, name="rs%d" % tn, tag="rs%d" % tn)
                 nc.vector.tensor_reduce(out=ms[:], in_=ss[:, 16 * tn : ss_next[tn]], axis=AX.X, op=ALU.add)
                 nc.scalar.activation(out=sd[:], in_=ms[:], func=ACT.Sqrt, bias=eps_t[:], scale=1.0)
-            for col in cols:
-                for k0 in range(0, uw, sub):
-                    a = (col + k0) % TILE_N
-                    nc.vector.tensor_tensor(
-                        out=o[:, col + k0 : col + k0 + sub], in0=w_of[col][:, k0 : k0 + sub], in1=cos2[:, a : a + sub], op=ALU.mult
-                    )
-                nc.gpsimd.tensor_tensor(
-                    out=o[:, col : col + uw], in0=o[:, col : col + uw], in1=s_of[col][:, 0:uw], op=ALU.add
+            for col in pair:
+                a = col % TILE_N
+                s = work.tile([P, TILE_N], F32, name="s", tag="s", bufs=4)
+                nc.vector.tensor_tensor(
+                    out=paired(s[:, 0:width]),
+                    in0=swapped(w_of[col][:, 0:width]),
+                    in1=paired(sin2[:, a : a + width] if tn == 0 else gsin[:, col : col + width]),
+                    op=ALU.mult,
                 )
+                s_of[col] = s
             if closing:
                 nc.vector.reciprocal(out=rs[:], in_=sd[:])
                 for lo in range(0, c0, 1024):
                     scale_on_scalar(tn, rs, lo, min(lo + 1024, c0))
-                if uw >= TILE_N:
-                    for col in cols:
-                        scale_on_scalar(tn, rs, col, col + uw)
-                else:
-                    scale_on_scalar(tn, rs, c0, c0 + n)
+            for col in pair:
+                nc.vector.tensor_tensor(
+                    out=o[:, col : col + width], in0=o[:, col : col + width], in1=s_of[col][:, 0:width], op=ALU.add
+                )
+            if closing:
+                nc.vector.tensor_scalar(out=o[:, c0:DIM], in0=o[:, c0:DIM], scalar1=rs[:], scalar2=None, op0=ALU.mult)
 
         def store(tn, blk):
             nc.sync.dma_start(out=outs[tn][:, 1024 * blk : 1024 * (blk + 1)], in_=res[tn][:, 1024 * blk : 1024 * (blk + 1)])
 
         for i in range(len(pieces)):
-            if i + LOOKAHEAD < len(pieces):
-                load_piece(i + LOOKAHEAD)
-            if i + LOOKAHEAD == len(pieces):
-                for blk in range(4):
-                    store(0, blk)
             if i < len(TABLE_PLAN):
                 for v, h in TABLE_PLAN[i]:
-                    spread(v, h)
-            if i == 2:
-                nc.tensor.matmul(out=cos2[:], lhsT=identf[:], rhs=cos_sb[:], start=True, stop=True)
+                    spread(v, h, tabs[v])
             run_passes(i)
             ci, g0, gp = pieces[i]
             if g0 + gp == GROUPS:
                 epilogue(ci)
+            for j in range(len(pieces)):
+                if emit_after[j] == i:
+                    load_piece(j)
+                    for blk in STORE_AFTER.get(j, ()):
+                        store(0, blk)
         for blk in range(4):
             store(1, blk)

@@ -108,16 +108,16 @@ def tile_selfattention_pa_kernel(
         psum = ctx.enter_context(tc.psum_pool(name="psum", bufs=8))
         ctx.enter_context(tc.manual_schedule())
 
-        rows = const.tile([P, TILE_N], BF16, name="rows", tag="rows")
+        rows = const.tile([P, TILE_N], BF16, name="rows", tag="rows", align_bytes=256)
         warm = const.tile([P, 2], F32, name="warm", tag="warm")
         eps_t = const.tile([P, 1], F32, name="eps_t", tag="eps_t")
-        xw = const.tile([P, GROUPS, 256], U8, name="xw", tag="xw", align_bytes=64)
-        xs = const.tile([P, GROUPS, P], U8, name="xs", tag="xs", align_bytes=64)
+        xw = const.tile([P, GROUPS, 256], U8, name="xw", tag="xw", align_bytes=256)
+        xs = const.tile([P, GROUPS, P], U8, name="xs", tag="xs", align_bytes=256)
         planes = []
         for a in range(SETS):
-            pl = const.tile([P, GROUPS, STRETCH], U8, name="pl%d" % a, tag="pl%d" % a, align_bytes=64)
+            pl = const.tile([P, GROUPS, STRETCH], U8, name="pl%d" % a, tag="pl%d" % a, align_bytes=256)
             planes.append(pl)
-        fr = const.tile([P, HALF], BF16, name="fr", tag="fr")
+        fr = const.tile([P, HALF], BF16, name="fr", tag="fr", align_bytes=256)
         ident = const.tile([P, P], BF16, name="ident", tag="ident")
         tabs = []
         for v in range(3):
@@ -125,7 +125,7 @@ def tile_selfattention_pa_kernel(
             tabs.append(tab)
         res = []
         for tn in range(2):
-            o = const.tile([P, DIM], F32, name="res%d" % tn, tag="res%d" % tn)
+            o = const.tile([P, DIM], F32, name="res%d" % tn, tag="res%d" % tn, align_bytes=256)
             res.append(o)
         ss = const.tile([P, 32], F32, name="ss", tag="ss")
         cos2 = const.tile([P, TILE_N], F32, name="cos2", tag="cos2")
@@ -164,7 +164,7 @@ def tile_selfattention_pa_kernel(
                 load_scale_row(st, r)
             ci, g0, gp = pieces[j]
             tn, c0, n = CHUNKS[ci][0:3]
-            wc = codes.tile([P, gp, 2 * n], U8, name="wc", tag="wc", align_bytes=64)
+            wc = codes.tile([P, gp, 2 * n], U8, name="wc", tag="wc", align_bytes=256)
             nc.sync.dma_start(
                 out=wc[:].bitcast(I32),
                 in_=w_words[tn][g0 : g0 + gp, :, 2 * c0 : 2 * (c0 + n)].rearrange("g p b -> p g b").bitcast(I32),

@@ -39,9 +39,8 @@ CHUNKS = (
 LAST_CHUNK = (3, 8)
 
 BEFORE = {
-    1: ((0, 1),),
-    2: ((0, 2), (1, 0)),
-    3: ((0, 3), (1, 1)),
+    2: ((1, 0),),
+    3: ((1, 1),),
     4: ((1, 2), (2, 0)),
     5: ((1, 3), (2, 1)),
     6: ((2, 2),),
@@ -137,8 +136,8 @@ def tile_selfattention_pa_kernel(
             nc.scalar.dma_start(out=rows[8 * v : 8 * v + 8, :], in_=vec.rearrange("(s n) -> s n", n=TILE_N))
         nc.scalar.dma_start(out=fr[:], in_=freqs.rearrange("s o j -> s (o j)"))
 
-        nc.vector.memset(planes[0][:].bitcast(I32), 0)
         nc.vector.memset(xs[:].bitcast(I32), 0)
+        nc.vector.memset(planes[0][:].bitcast(I32), 0)
         nc.vector.memset(warm[:], 0.0)
         nc.vector.memset(rows[32:64, :], 0.0)
         nc.vector.memset(rows[64:128, :], 0.0)
@@ -154,10 +153,11 @@ def tile_selfattention_pa_kernel(
 
         def load_scale_row(st, r):
             src = w_scales[st // 2][:, :, STRETCH * (st % 2) : STRETCH * (st % 2 + 1)]
-            nc.sync.dma_start(
-                out=planes[st % SETS][r:P:32].bitcast(I32),
-                in_=src[:, r:16:4, :].rearrange("g q n -> q g n").bitcast(I32),
-            )
+            for quad in (0, 2, 1, 3):
+                nc.sync.dma_start(
+                    out=planes[st % SETS][32 * quad + r : 32 * quad + r + 1].bitcast(I32),
+                    in_=src[:, 4 * quad + r : 4 * quad + r + 1, :].rearrange("g q n -> q g n").bitcast(I32),
+                )
 
         def load_piece(j):
             for st, r in BEFORE.get(j, ()):
@@ -185,13 +185,15 @@ def tile_selfattention_pa_kernel(
             nc.scalar.copy(out=dst[:, 1024 * h : 1024 * (h + 1)], in_=bank[:])
 
         nc.sync.dma_start(out=xw[:].bitcast(I32), in_=x_words.rearrange("g p b -> p g b").bitcast(I32))
-        load_scale_row(0, 0)
+        load_piece(0)
         for quad in range(4):
             nc.sync.dma_start(
                 out=xs[32 * quad : 32 * quad + 4].bitcast(I32),
                 in_=x_scales[:, 4 * quad : 4 * quad + 4, :].rearrange("g r n -> r g n").bitcast(I32),
             )
-        for j in range(len(pieces)):
+        for r in range(4):
+            load_scale_row(0, r)
+        for j in range(1, len(pieces)):
             if emit_after[j] < 0:
                 load_piece(j)
 

@@ -229,6 +229,7 @@ def tile_selfattention_pa_kernel(
             nc.scalar.activation(out=pm[:, 1, :], in_=rd[:], func=ACT.Sin)
             nc.scalar.activation(out=cc[:, 0, :], in_=ab[:], func=ACT.Sin)
             nc.scalar.activation(out=cc[:, 1, :], in_=ab[:], func=ACT.Sin)
+            nc.scalar.activation(out=warm[:, 1:2], in_=eps_t[:], func=ACT.Abs_reciprocal_sqrt)
             nc.vector.tensor_copy(out=paired(sin2[:]), in_=pm[:].rearrange("p e j -> p j e"))
             nc.vector.tensor_copy(out=paired(cos2[:]), in_=cc[:].rearrange("p e j -> p j e"))
 
@@ -275,15 +276,18 @@ def tile_selfattention_pa_kernel(
         def scale_on_scalar(tn, rs, lo, hi):
             nc.scalar.activation(out=res[tn][:, lo:hi], in_=res[tn][:, lo:hi], func=ACT.Copy, scale=rs[:])
 
-        def epilogue(ci):
+        t_of = {}
+        s_of = {}
+        rs_of = {}
+
+        def columns(ci):
             tn, c0, n = CHUNKS[ci][0:3]
             width = min(TILE_N, n // 2)
-            o = res[tn]
-            pair = (c0, c0 + width)
-            closing = ci in LAST_CHUNK
-            t_of = {}
-            w_of = {}
-            s_of = {}
+            return tn, width, (c0, c0 + width)
+
+        def sums(ci):
+            tn, width, pair = columns(ci)
+            c0 = CHUNKS[ci][1]
             for col in pair:
                 acc = banks[ci][(col - c0) // TILE_N]
                 b0 = (col - c0) % TILE_N
@@ -300,53 +304,92 @@ def tile_selfattention_pa_kernel(
                     accum_out=ss[:, ss_next[tn] : ss_next[tn] + 1],
                 )
                 ss_next[tn] += 1
-                t_of[col] = t
-            for col in pair:
-                if tn == 0:
+                t_of[(tn, col)] = t
+
+        def inverse_rms(tn):
+            ms = const.tile([P, 1], F32, name="ms%d" % tn, tag="ms%d" % tn)
+            sc = const.tile([P, 16], F32, name="sc%d" % tn, tag="sc%d" % tn)
+            rs = const.tile([P, 1], F32, name="rs%d" % tn, tag="rs%d" % tn)
+            nc.scalar.activation(
+                out=sc[:, 0 : ss_next[tn] - 16 * tn], in_=ss[:, 16 * tn : ss_next[tn]], func=ACT.Copy, accum_out=ms[:]
+            )
+            nc.scalar.activation(out=rs[:], in_=ms[:], func=ACT.Abs_reciprocal_sqrt, bias=eps_t[:], scale=1.0)
+            rs_of[tn] = rs
+
+        def times(out, in0, in1, rs):
+            if rs is None:
+                nc.vector.tensor_tensor(out=out, in0=in0, in1=in1, op=ALU.mult)
+            else:
+                nc.vector.scalar_tensor_tensor(out=out, in0=in0, scalar=rs[:], in1=in1, op0=ALU.mult, op1=ALU.mult)
+
+        def products(ci, rs):
+            tn, width, pair = columns(ci)
+            o = res[tn]
+            if tn == 0:
+                for col in pair:
                     w = work.tile([P, TILE_N], F32, name="w", tag="w", bufs=4)
-                    nc.vector.tensor_tensor(
-                        out=w[:, 0:width], in0=t_of[col][:, 0:width], in1=tabs[1][:, col : col + width], op=ALU.mult
-                    )
-                    w_of[col] = w
-                else:
-                    w_of[col] = t_of[col]
+                    times(w[:, 0:width], t_of[(tn, col)][:, 0:width], tabs[1][:, col : col + width], rs)
+                    t_of[(tn, col)] = w
+                rs = None
             for col in pair:
                 a = col % TILE_N
-                nc.vector.tensor_tensor(
-                    out=o[:, col : col + width],
-                    in0=w_of[col][:, 0:width],
-                    in1=cos2[:, a : a + width] if tn == 0 else gcos[:, col : col + width],
-                    op=ALU.mult,
+                times(
+                    o[:, col : col + width],
+                    t_of[(tn, col)][:, 0:width],
+                    cos2[:, a : a + width] if tn == 0 else gcos[:, col : col + width],
+                    rs,
                 )
-            if closing:
-                ms = const.tile([P, 1], F32, name="ms%d" % tn, tag="ms%d" % tn)
-                sd = const.tile([P, 1], F32, name="sd%d" % tn, tag="sd%d" % tn)
-                rs = const.tile([P, 1], F32, name="rs%d" % tn, tag="rs%d" % tn)
-                nc.vector.tensor_reduce(out=ms[:], in_=ss[:, 16 * tn : ss_next[tn]], axis=AX.X, op=ALU.add)
-                nc.scalar.activation(out=sd[:], in_=ms[:], func=ACT.Sqrt, bias=eps_t[:], scale=1.0)
             for col in pair:
                 a = col % TILE_N
                 s = work.tile([P, TILE_N], F32, name="s", tag="s", bufs=4)
-                nc.vector.tensor_tensor(
-                    out=paired(s[:, 0:width]),
-                    in0=swapped(w_of[col][:, 0:width]),
-                    in1=paired(sin2[:, a : a + width] if tn == 0 else gsin[:, col : col + width]),
-                    op=ALU.mult,
+                times(
+                    paired(s[:, 0:width]),
+                    swapped(t_of[(tn, col)][:, 0:width]),
+                    paired(sin2[:, a : a + width] if tn == 0 else gsin[:, col : col + width]),
+                    rs,
                 )
-                s_of[col] = s
-            if closing:
-                nc.vector.reciprocal(out=rs[:], in_=sd[:])
-                for lo in range(0, c0, 1024):
-                    scale_on_scalar(tn, rs, lo, min(lo + 1024, c0))
+                s_of[(tn, col)] = s
+
+        def adds(ci):
+            tn, width, pair = columns(ci)
+            o = res[tn]
             for col in pair:
                 nc.vector.tensor_tensor(
-                    out=o[:, col : col + width], in0=o[:, col : col + width], in1=s_of[col][:, 0:width], op=ALU.add
+                    out=o[:, col : col + width], in0=o[:, col : col + width], in1=s_of[(tn, col)][:, 0:width], op=ALU.add
                 )
-            if closing:
-                nc.vector.tensor_scalar(out=o[:, c0:DIM], in0=o[:, c0:DIM], scalar1=rs[:], scalar2=None, op0=ALU.mult)
 
-        def store(tn, blk):
-            nc.sync.dma_start(out=outs[tn][:, 1024 * blk : 1024 * (blk + 1)], in_=res[tn][:, 1024 * blk : 1024 * (blk + 1)])
+        def store(tn, c0, n):
+            nc.sync.dma_start(out=outs[tn][:, c0 : c0 + n], in_=res[tn][:, c0 : c0 + n])
+
+        def epilogue(ci):
+            if ci < 3 or ci in (4, 5):
+                sums(ci)
+                products(ci, None)
+                adds(ci)
+            elif ci == 3:
+                sums(3)
+                inverse_rms(0)
+                for lo in range(0, 3072, 1024):
+                    scale_on_scalar(0, rs_of[0], lo, lo + 1024)
+                products(3, None)
+                adds(3)
+                scale_on_scalar(0, rs_of[0], 3072, DIM)
+            elif ci == 6:
+                sums(6)
+            elif ci == 7:
+                sums(7)
+                products(6, None)
+            else:
+                sums(8)
+                inverse_rms(1)
+                adds(6)
+                for lo in range(0, 3072, 1024):
+                    scale_on_scalar(1, rs_of[1], lo, lo + 1024)
+                    store(1, lo, 1024)
+                for cj in (7, 8):
+                    products(cj, rs_of[1])
+                    adds(cj)
+                    store(1, CHUNKS[cj][1], CHUNKS[cj][2])
 
         for i in range(len(pieces)):
             if i < len(TABLE_PLAN):
@@ -360,6 +403,4 @@ def tile_selfattention_pa_kernel(
                 if emit_after[j] == i:
                     load_piece(j)
                     for blk in STORE_AFTER.get(j, ()):
-                        store(0, blk)
-        for blk in range(4):
-            store(1, blk)
+                        store(0, 1024 * blk, 1024)

@@ -24,6 +24,7 @@ STRETCH = 2048
 SETS = 3
 EPS = 1e-6
 LOOKAHEAD = 4
+FOLD_N = 2048
 
 CHUNKS = (
     (0, 0, 1024, (4, 4)),
@@ -52,10 +53,9 @@ BEFORE = {
 }
 STORE_AFTER = {17: (0, 1, 2, 3)}
 
-HEAD_TABLES = ((3, 0), (3, 1), (3, 2), (3, 3), (0, 0), (1, 0))
+FIRST_TABLES = ((3, 0), (3, 1))
+HEAD_TABLES = ((3, 2), (3, 3), (0, 0), (1, 0), (0, 1), (1, 1), (0, 2), (1, 2))
 TABLE_PLAN = (
-    ((0, 1), (1, 1)),
-    ((0, 2), (1, 2)),
     ((0, 3), (1, 3)),
     ((2, 0), (2, 1)),
     ((2, 2), (2, 3)),
@@ -138,10 +138,10 @@ def tile_selfattention_pa_kernel(
 
         nc.vector.memset(xs[:].bitcast(I32), 0)
         nc.vector.memset(planes[0][:].bitcast(I32), 0)
-        nc.vector.memset(warm[:], 0.0)
-        nc.vector.memset(rows[32:64, :], 0.0)
-        nc.vector.memset(rows[64:128, :], 0.0)
-        nc.vector.memset(eps_t[:], EPS)
+        nc.gpsimd.memset(warm[:], 0.0)
+        nc.gpsimd.memset(rows[32:64, :], 0.0)
+        nc.gpsimd.memset(rows[64:128, :], 0.0)
+        nc.gpsimd.memset(eps_t[:], EPS)
         make_identity(nc, ident[:])
         for a in range(1, SETS):
             for g in range(0, GROUPS, 2):
@@ -199,7 +199,7 @@ def tile_selfattention_pa_kernel(
 
         with tc.tile_pool(name="head", bufs=1) as head:
             gk_tab = head.tile([P, DIM], BF16, name="gk_tab", tag="gk_tab")
-            for v, h in HEAD_TABLES:
+            for v, h in FIRST_TABLES:
                 spread(v, h, gk_tab if v == 3 else tabs[v])
 
             two_pi = 2.0 * math.pi
@@ -214,7 +214,7 @@ def tile_selfattention_pa_kernel(
             rd = head.tile([P, HALF], F32, name="rd", tag="rd")
             ab = head.tile([P, HALF], F32, name="ab", tag="ab")
             pm = head.tile([P, 2, HALF], F32, name="pm", tag="pm")
-            cc = head.tile([P, 2, HALF], F32, name="cc", tag="cc")
+            cc = head.tile([P, HALF], F32, name="cc", tag="cc")
             nc.vector.tensor_scalar(out=ki[:], in0=fr[:], scalar1=1.0 / two_pi, scalar2=None, op0=ALU.mult)
             nc.vector.tensor_copy(out=kf[:], in_=ki[:])
             nc.vector.scalar_tensor_tensor(out=ra[:], in0=kf[:], scalar=-c_hi, in1=fr[:], op0=ALU.mult, op1=ALU.add)
@@ -227,20 +227,25 @@ def tile_selfattention_pa_kernel(
             nc.vector.tensor_scalar(out=ab[:], in0=ma[:], scalar1=0.5 * math.pi, scalar2=None, op0=ALU.add)
             nc.scalar.activation(out=pm[:, 0, :], in_=rd[:], func=ACT.Sin, scale=-1.0)
             nc.scalar.activation(out=pm[:, 1, :], in_=rd[:], func=ACT.Sin)
-            nc.scalar.activation(out=cc[:, 0, :], in_=ab[:], func=ACT.Sin)
-            nc.scalar.activation(out=cc[:, 1, :], in_=ab[:], func=ACT.Sin)
+            nc.scalar.activation(out=cc[:], in_=ab[:], func=ACT.Sin)
+            for v, h in HEAD_TABLES:
+                spread(v, h, gk_tab if v == 3 else tabs[v])
             nc.scalar.activation(out=warm[:, 1:2], in_=eps_t[:], func=ACT.Abs_reciprocal_sqrt)
             nc.vector.tensor_copy(out=paired(sin2[:]), in_=pm[:].rearrange("p e j -> p j e"))
-            nc.vector.tensor_copy(out=paired(cos2[:]), in_=cc[:].rearrange("p e j -> p j e"))
+            nc.vector.tensor_copy(out=paired(cos2[:]), in_=cc[:].unsqueeze(2).to_broadcast([P, HALF, 2]))
 
-            for col in range(0, DIM, TILE_N):
+            for col in range(0, DIM, FOLD_N):
+                heads = FOLD_N // TILE_N
                 nc.vector.tensor_tensor(
-                    out=gcos[:, col : col + TILE_N], in0=gk_tab[:, col : col + TILE_N], in1=cos2[:], op=ALU.mult
+                    out=gcos[:, col : col + FOLD_N].rearrange("p (h n) -> p h n", h=heads),
+                    in0=gk_tab[:, col : col + FOLD_N].rearrange("p (h n) -> p h n", h=heads),
+                    in1=cos2[:].unsqueeze(1).to_broadcast([P, heads, TILE_N]),
+                    op=ALU.mult,
                 )
                 nc.vector.tensor_tensor(
-                    out=paired(gsin[:, col : col + TILE_N]),
-                    in0=swapped(gk_tab[:, col : col + TILE_N]),
-                    in1=paired(sin2[:]),
+                    out=gsin[:, col : col + FOLD_N].rearrange("p (h j e) -> p h j e", h=heads, e=2),
+                    in0=gk_tab[:, col : col + FOLD_N].rearrange("p (h j e) -> p h j e", h=heads, e=2)[:, :, :, ::-1],
+                    in1=paired(sin2[:]).unsqueeze(1).to_broadcast([P, heads, HALF, 2]),
                     op=ALU.mult,
                 )
 
@@ -382,8 +387,18 @@ def tile_selfattention_pa_kernel(
             else:
                 sums(8)
                 inverse_rms(1)
+                scale_on_scalar(1, rs_of[1], 0, TILE_N)
+                store(1, 0, TILE_N)
+                nc.vector.tensor_scalar(
+                    out=res[1][:, TILE_N : 2 * TILE_N],
+                    in0=res[1][:, TILE_N : 2 * TILE_N],
+                    scalar1=rs_of[1][:],
+                    scalar2=None,
+                    op0=ALU.mult,
+                )
+                store(1, TILE_N, TILE_N)
                 adds(6)
-                for lo in range(0, 3072, 1024):
+                for lo in range(1024, 3072, 1024):
                     scale_on_scalar(1, rs_of[1], lo, lo + 1024)
                     store(1, lo, 1024)
                 for cj in (7, 8):

@@ -327,7 +327,7 @@ def tile_selfattention_pa_kernel(
             else:
                 nc.vector.scalar_tensor_tensor(out=out, in0=in0, scalar=rs[:], in1=in1, op0=ALU.mult, op1=ALU.mult)
 
-        def products(ci, rs):
+        def cosines(ci, rs):
             tn, width, pair = columns(ci)
             o = res[tn]
             if tn == 0:
@@ -344,6 +344,9 @@ def tile_selfattention_pa_kernel(
                     cos2[:, a : a + width] if tn == 0 else gcos[:, col : col + width],
                     rs,
                 )
+
+        def sines(ci, rs):
+            tn, width, pair = columns(ci)
             for col in pair:
                 a = col % TILE_N
                 s = work.tile([P, TILE_N], F32, name="s", tag="s", bufs=4)
@@ -369,26 +372,29 @@ def tile_selfattention_pa_kernel(
         def epilogue(ci):
             if ci < 3 or ci in (4, 5):
                 sums(ci)
-                products(ci, None)
+                cosines(ci, None)
+                sines(ci, None)
                 adds(ci)
             elif ci == 3:
                 sums(3)
                 inverse_rms(0)
                 for lo in range(0, 3072, 1024):
                     scale_on_scalar(0, rs_of[0], lo, lo + 1024)
-                products(3, None)
+                cosines(3, None)
+                sines(3, None)
                 adds(3)
                 scale_on_scalar(0, rs_of[0], 3072, DIM)
             elif ci == 6:
                 sums(6)
+                cosines(6, None)
             elif ci == 7:
                 sums(7)
-                products(6, None)
             else:
                 sums(8)
                 inverse_rms(1)
                 scale_on_scalar(1, rs_of[1], 0, TILE_N)
                 store(1, 0, TILE_N)
+                sines(6, None)
                 nc.vector.tensor_scalar(
                     out=res[1][:, TILE_N : 2 * TILE_N],
                     in0=res[1][:, TILE_N : 2 * TILE_N],
@@ -402,7 +408,8 @@ def tile_selfattention_pa_kernel(
                     scale_on_scalar(1, rs_of[1], lo, lo + 1024)
                     store(1, lo, 1024)
                 for cj in (7, 8):
-                    products(cj, rs_of[1])
+                    cosines(cj, rs_of[1])
+                    sines(cj, rs_of[1])
                     adds(cj)
                     store(1, CHUNKS[cj][1], CHUNKS[cj][2])
 

@@ -33,8 +33,8 @@ CHUNKS = (
     (0, 3072, 1024, (4, 4)),
     (1, 0, 1024, (4, 4)),
     (1, 1024, 1024, (4, 4)),
-    (1, 2048, 1024, (4, 4)),
-    (1, 3072, 512, (8,)),
+    (1, 2048, 1024, (4, 2, 2)),
+    (1, 3072, 512, (4, 4)),
     (1, 3584, 512, (4, 2, 2)),
 )
 LAST_CHUNK = (3, 8)
@@ -51,7 +51,7 @@ BEFORE = {
     11: ((3, 2),),
     12: ((3, 3),),
 }
-STORE_AFTER = {17: (0, 1, 2, 3)}
+STORE_AFTER = {19: (0, 1, 2, 3)}
 
 FIRST_TABLES = ((3, 0), (3, 1))
 HEAD_TABLES = ((3, 2), (3, 3), (0, 0), (1, 0), (0, 1), (1, 1), (0, 2), (1, 2))

from contextlib import ExitStack
import math

import concourse.mybir as mybir
from concourse.masks import make_identity

FLOPS = 2 * 128 * 4096 * 8192

F32 = mybir.dt.float32
BF16 = mybir.dt.bfloat16
U8 = mybir.dt.uint8
I32 = mybir.dt.int32
FP4X4 = mybir.dt.float4_e2m1fn_x4
ALU = mybir.AluOpType
ACT = mybir.ActivationFunctionType
AX = mybir.AxisListType

P = 128
DIM = 4096
GROUPS = 8
TILE_N = 512
HALF = 256
STRETCH = 2048
SETS = 3
EPS = 1e-6
LOOKAHEAD = 4
FOLD_N = 2048

CHUNKS = (
    (0, 0, 1024, (4, 4)),
    (0, 1024, 1024, (4, 4)),
    (0, 2048, 1024, (4, 4)),
    (0, 3072, 1024, (4, 4)),
    (1, 0, 1024, (4, 4)),
    (1, 1024, 1024, (4, 4)),
    (1, 2048, 1024, (4, 2, 2)),
    (1, 3072, 512, (4, 4)),
    (1, 3584, 512, (4, 2, 2)),
)
LAST_CHUNK = (3, 8)

BEFORE = {
    2: ((1, 0),),
    3: ((1, 1),),
    4: ((1, 2), (2, 0)),
    5: ((1, 3), (2, 1)),
    6: ((2, 2),),
    7: ((2, 3),),
    9: ((3, 0),),
    10: ((3, 1),),
    11: ((3, 2),),
    12: ((3, 3),),
}
STORE_AFTER = {19: (0, 1, 2, 3)}

FIRST_TABLES = ((3, 0), (3, 1))
HEAD_TABLES = ((3, 2), (3, 3), (0, 0), (1, 0), (0, 1), (1, 1), (0, 2), (1, 2))
TABLE_PLAN = (
    ((0, 3), (1, 3)),
    ((2, 0), (2, 1)),
    ((2, 2), (2, 3)),
)


def swapped(ap):
    return ap.rearrange("p (j e) -> p j e", e=2)[:, :, ::-1]


def paired(ap):
    return ap.rearrange("p (j e) -> p j e", e=2)


def tile_selfattention_pa_kernel(
    tc, x_words, x_scales, freqs, Wq_words, Wq_scales, bq, Wk_words, Wk_scales, bk, gq, gk, out_0, out_1
):
    nc = tc.nc
    w_words = (Wq_words, Wk_words)
    w_scales = (Wq_scales, Wk_scales)
    outs = (out_0.rearrange("b s d -> (b s) d"), out_1.rearrange("b s d -> (b s) d"))

    pieces = []
    for ci, chunk in enumerate(CHUNKS):
        g0 = 0
        for gp in chunk[3]:
            pieces.append((ci, g0, gp))
            g0 += gp

    first_piece = {}
    last_piece = {}
    for j, piece in enumerate(pieces):
        st = 2 * CHUNKS[piece[0]][0] + CHUNKS[piece[0]][1] // STRETCH
        first_piece.setdefault(st, j)
        last_piece[st] = j
    emit_after = {}
    floor = -1
    for j in range(len(pieces)):
        floor = max(floor, j - LOOKAHEAD)
        for st, r in BEFORE.get(j, ()):
            if st >= SETS:
                floor = max(floor, last_piece[st - SETS])
            assert floor < first_piece[st]
        emit_after[j] = floor

    with ExitStack() as ctx:
        const = ctx.enter_context(tc.tile_pool(name="const", bufs=1))
        codes = ctx.enter_context(tc.tile_pool(name="codes", bufs=6))
        psum = ctx.enter_context(tc.psum_pool(name="psum", bufs=8))
        ctx.enter_context(tc.manual_schedule())

        rows = const.tile([P, TILE_N], BF16, name="rows", tag="rows", align_bytes=256)
        warm = const.tile([P, 2], F32, name="warm", tag="warm")
        eps_t = const.tile([P, 1], F32, name="eps_t", tag="eps_t")
        xw = const.tile([P, GROUPS, 256], U8, name="xw", tag="xw", align_bytes=256)
        xs = const.tile([P, GROUPS, P], U8, name="xs", tag="xs", align_bytes=256)
        planes = []
        for a in range(SETS):
            pl = const.tile([P, GROUPS, STRETCH], U8, name="pl%d" % a, tag="pl%d" % a, align_bytes=256)
            planes.append(pl)
        fr = const.tile([P, HALF], BF16, name="fr", tag="fr", align_bytes=256)
        ident = const.tile([P, P], BF16, name="ident", tag="ident")
        tabs = []
        for v in range(3):
            tab = const.tile([P, DIM], BF16, name="tab%d" % v, tag="tab%d" % v)
            tabs.append(tab)
        res = []
        for tn in range(2):
            o = const.tile([P, DIM], F32, name="res%d" % tn, tag="res%d" % tn, align_bytes=256)
            res.append(o)
        ss = const.tile([P, 32], F32, name="ss", tag="ss")
        cos2 = const.tile([P, TILE_N], F32, name="cos2", tag="cos2")
        sin2 = const.tile([P, TILE_N], F32, name="sin2", tag="sin2")
        gcos = const.tile([P, DIM], F32, name="gcos", tag="gcos")
        gsin = const.tile([P, DIM], F32, name="gsin", tag="gsin")

        for v, vec in enumerate((bq, gq, bk, gk)):
            nc.scalar.dma_start(out=rows[8 * v : 8 * v + 8, :], in_=vec.rearrange("(s n) -> s n", n=TILE_N))
        nc.scalar.dma_start(out=fr[:], in_=freqs.rearrange("s o j -> s (o j)"))

        nc.vector.memset(xs[:].bitcast(I32), 0)
        nc.vector.memset(planes[0][:].bitcast(I32), 0)
        nc.gpsimd.memset(warm[:], 0.0)
        nc.gpsimd.memset(rows[32:64, :], 0.0)
        nc.gpsimd.memset(rows[64:128, :], 0.0)
        nc.gpsimd.memset(eps_t[:], EPS)
        make_identity(nc, ident[:])
        for a in range(1, SETS):
            for g in range(0, GROUPS, 2):
                nc.gpsimd.memset(planes[a][:, g : g + 2].bitcast(F32), 0.0)
        nc.scalar.activation(out=warm[:, 1:2], in_=warm[:, 0:1], func=ACT.Sin)

        code_tiles = {}
        banks = {}

        def load_scale_row(st, r):
            src = w_scales[st // 2][:, :, STRETCH * (st % 2) : STRETCH * (st % 2 + 1)]
            for quad in (0, 2, 1, 3):
                nc.sync.dma_start(
                    out=planes[st % SETS][32 * quad + r : 32 * quad + r + 1].bitcast(I32),
                    in_=src[:, 4 * quad + r : 4 * quad + r + 1, :].rearrange("g q n -> q g n").bitcast(I32),
                )

        def load_piece(j):
            for st, r in BEFORE.get(j, ()):
                load_scale_row(st, r)
            ci, g0, gp = pieces[j]
            tn, c0, n = CHUNKS[ci][0:3]
            wc = codes.tile([P, gp, 2 * n], U8, name="wc", tag="wc", align_bytes=256)
            nc.sync.dma_start(
                out=wc[:].bitcast(I32),
                in_=w_words[tn][g0 : g0 + gp, :, 2 * c0 : 2 * (c0 + n)].rearrange("g p b -> p g b").bitcast(I32),
            )
            code_tiles[j] = wc

        def spread(v, h, dst):
            bank = psum.tile([P, 2 * TILE_N], BF16, name="tb", tag="bank")
            for u in range(2):
                r = 8 * v + 2 * h + u
                nc.tensor.matmul(
                    out=bank[:, TILE_N * u : TILE_N * (u + 1)],
                    lhsT=ident[:, r : r + 1].to_broadcast([P, P]),
                    rhs=rows[:],
                    start=True,
                    stop=True,
                )
            nc.scalar.copy(out=dst[:, 1024 * h : 1024 * (h + 1)], in_=bank[:])

        nc.sync.dma_start(out=xw[:].bitcast(I32), in_=x_words.rearrange("g p b -> p g b").bitcast(I32))
        load_piece(0)
        for quad in range(4):
            nc.sync.dma_start(
                out=xs[32 * quad : 32 * quad + 4].bitcast(I32),
                in_=x_scales[:, 4 * quad : 4 * quad + 4, :].rearrange("g r n -> r g n").bitcast(I32),
            )
        for r in range(4):
            load_scale_row(0, r)
        for j in range(1, len(pieces)):
            if emit_after[j] < 0:
                load_piece(j)

        with tc.tile_pool(name="head", bufs=1) as head:
            gk_tab = head.tile([P, DIM], BF16, name="gk_tab", tag="gk_tab")
            for v, h in FIRST_TABLES:
                spread(v, h, gk_tab if v == 3 else tabs[v])

            two_pi = 2.0 * math.pi
            c_hi = 6.28125
            c_lo = two_pi - c_hi
            ki = head.tile([P, HALF], I32, name="ki", tag="ki")
            kf = head.tile([P, HALF], F32, name="kf", tag="kf")
            ra = head.tile([P, HALF], F32, name="ra", tag="ra")
            rb = head.tile([P, HALF], F32, name="rb", tag="rb")
            ma = head.tile([P, HALF], F32, name="ma", tag="ma")
            mb = head.tile([P, HALF], F32, name="mb", tag="mb")
            rd = head.tile([P, HALF], F32, name="rd", tag="rd")
            ab = head.tile([P, HALF], F32, name="ab", tag="ab")
            pm = head.tile([P, 2, HALF], F32, name="pm", tag="pm")
            cc = head.tile([P, HALF], F32, name="cc", tag="cc")
            nc.vector.tensor_scalar(out=ki[:], in0=fr[:], scalar1=1.0 / two_pi, scalar2=None, op0=ALU.mult)
            nc.vector.tensor_copy(out=kf[:], in_=ki[:])
            nc.vector.scalar_tensor_tensor(out=ra[:], in0=kf[:], scalar=-c_hi, in1=fr[:], op0=ALU.mult, op1=ALU.add)
            nc.vector.scalar_tensor_tensor(out=rb[:], in0=kf[:], scalar=-c_lo, in1=ra[:], op0=ALU.mult, op1=ALU.add)
            nc.vector.tensor_scalar(out=ma[:], in0=rb[:], scalar1=math.pi, scalar2=-two_pi, op0=ALU.is_gt, op1=ALU.mult)
            nc.vector.tensor_scalar(out=mb[:], in0=rb[:], scalar1=-math.pi, scalar2=two_pi, op0=ALU.is_lt, op1=ALU.mult)
            nc.vector.tensor_tensor(out=ra[:], in0=rb[:], in1=ma[:], op=ALU.add)
            nc.vector.tensor_tensor(out=rd[:], in0=ra[:], in1=mb[:], op=ALU.add)
            nc.vector.scalar_tensor_tensor(out=ma[:], in0=rd[:], scalar=-1.0, in1=rd[:], op0=ALU.mult, op1=ALU.min)
            nc.vector.tensor_scalar(out=ab[:], in0=ma[:], scalar1=0.5 * math.pi, scalar2=None, op0=ALU.add)
            nc.scalar.activation(out=pm[:, 0, :], in_=rd[:], func=ACT.Sin, scale=-1.0)
            nc.scalar.activation(out=pm[:, 1, :], in_=rd[:], func=ACT.Sin)
            nc.scalar.activation(out=cc[:], in_=ab[:], func=ACT.Sin)
            for v, h in HEAD_TABLES:
                spread(v, h, gk_tab if v == 3 else tabs[v])
            nc.scalar.activation(out=warm[:, 1:2], in_=eps_t[:], func=ACT.Abs_reciprocal_sqrt)
            nc.vector.tensor_copy(out=paired(sin2[:]), in_=pm[:].rearrange("p e j -> p j e"))
            nc.vector.tensor_copy(out=paired(cos2[:]), in_=cc[:].unsqueeze(2).to_broadcast([P, HALF, 2]))

            for col in range(0, DIM, FOLD_N):
                heads = FOLD_N // TILE_N
                nc.vector.tensor_tensor(
                    out=gcos[:, col : col + FOLD_N].rearrange("p (h n) -> p h n", h=heads),
                    in0=gk_tab[:, col : col + FOLD_N].rearrange("p (h n) -> p h n", h=heads),
                    in1=cos2[:].unsqueeze(1).to_broadcast([P, heads, TILE_N]),
                    op=ALU.mult,
                )
                nc.vector.tensor_tensor(
                    out=gsin[:, col : col + FOLD_N].rearrange("p (h j e) -> p h j e", h=heads, e=2),
                    in0=gk_tab[:, col : col + FOLD_N].rearrange("p (h j e) -> p h j e", h=heads, e=2)[:, :, :, ::-1],
                    in1=paired(sin2[:]).unsqueeze(1).to_broadcast([P, heads, HALF, 2]),
                    op=ALU.mult,
                )

        work = ctx.enter_context(tc.tile_pool(name="work", bufs=2))

        def run_passes(i):
            ci, g0, gp = pieces[i]
            tn, c0, n = CHUNKS[ci][0:3]
            if g0 == 0:
                accs = []
                for ti in range(n // TILE_N):
                    acc = psum.tile([P, TILE_N], F32, name="acc", tag="bank")
                    accs.append(acc)
                banks[ci] = accs
            plane = planes[(2 * tn + c0 // STRETCH) % SETS]
            pc = c0 % STRETCH
            wc = code_tiles[i]
            for gi in range(gp):
                g = g0 + gi
                for ti, acc in enumerate(banks[ci]):
                    nc.tensor.matmul_mx(
                        out=acc[:],
                        lhsT=xw[:, g, :].bitcast(FP4X4),
                        lhsT_scale=xs[:, g, :],
                        rhs=wc[:, gi, 2 * TILE_N * ti : 2 * TILE_N * (ti + 1)].bitcast(FP4X4),
                        rhs_scale=plane[:, g, pc + TILE_N * ti : pc + TILE_N * (ti + 1)],
                        start=(g == 0),
                        stop=(g == GROUPS - 1),
                    )

        ss_next = [0, 16]

        def scale_on_scalar(tn, rs, lo, hi):
            nc.scalar.activation(out=res[tn][:, lo:hi], in_=res[tn][:, lo:hi], func=ACT.Copy, scale=rs[:])

        t_of = {}
        s_of = {}
        rs_of = {}

        def columns(ci):
            tn, c0, n = CHUNKS[ci][0:3]
            width = min(TILE_N, n // 2)
            return tn, width, (c0, c0 + width)

        def sums(ci):
            tn, width, pair = columns(ci)
            c0 = CHUNKS[ci][1]
            for col in pair:
                acc = banks[ci][(col - c0) // TILE_N]
                b0 = (col - c0) % TILE_N
                t = work.tile([P, TILE_N], F32, name="t", tag="t", bufs=6)
                nc.vector.tensor_tensor(
                    out=t[:, 0:width], in0=acc[:, b0 : b0 + width], in1=tabs[2 * tn][:, col : col + width], op=ALU.add
                )
                junk = work.tile([P, TILE_N], F32, name="junk", tag="junk", bufs=2)
                nc.scalar.activation(
                    out=junk[:, 0:width],
                    in_=t[:, 0:width],
                    func=ACT.Square,
                    scale=1.0 / 64.0,
                    accum_out=ss[:, ss_next[tn] : ss_next[tn] + 1],
                )
                ss_next[tn] += 1
                t_of[(tn, col)] = t

        def inverse_rms(tn):
            ms = const.tile([P, 1], F32, name="ms%d" % tn, tag="ms%d" % tn)
            sc = const.tile([P, 16], F32, name="sc%d" % tn, tag="sc%d" % tn)
            rs = const.tile([P, 1], F32, name="rs%d" % tn, tag="rs%d" % tn)
            nc.scalar.activation(
                out=sc[:, 0 : ss_next[tn] - 16 * tn], in_=ss[:, 16 * tn : ss_next[tn]], func=ACT.Copy, accum_out=ms[:]
            )
            nc.scalar.activation(out=rs[:], in_=ms[:], func=ACT.Abs_reciprocal_sqrt, bias=eps_t[:], scale=1.0)
            rs_of[tn] = rs

        def times(out, in0, in1, rs):
            if rs is None:
                nc.vector.tensor_tensor(out=out, in0=in0, in1=in1, op=ALU.mult)
            else:
                nc.vector.scalar_tensor_tensor(out=out, in0=in0, scalar=rs[:], in1=in1, op0=ALU.mult, op1=ALU.mult)

        def cosines(ci, rs):
            tn, width, pair = columns(ci)
            o = res[tn]
            if tn == 0:
                for col in pair:
                    w = work.tile([P, TILE_N], F32, name="w", tag="w", bufs=4)
                    times(w[:, 0:width], t_of[(tn, col)][:, 0:width], tabs[1][:, col : col + width], rs)
                    t_of[(tn, col)] = w
                rs = None
            for col in pair:
                a = col % TILE_N
                times(
                    o[:, col : col + width],
                    t_of[(tn, col)][:, 0:width],
                    cos2[:, a : a + width] if tn == 0 else gcos[:, col : col + width],
                    rs,
                )

        def sines(ci, rs):
            tn, width, pair = columns(ci)
            for col in pair:
                a = col % TILE_N
                s = work.tile([P, TILE_N], F32, name="s", tag="s", bufs=4)
                times(
                    paired(s[:, 0:width]),
                    swapped(t_of[(tn, col)][:, 0:width]),
                    paired(sin2[:, a : a + width] if tn == 0 else gsin[:, col : col + width]),
                    rs,
                )
                s_of[(tn, col)] = s

        def adds(ci):
            tn, width, pair = columns(ci)
            o = res[tn]
            for col in pair:
                nc.vector.tensor_tensor(
                    out=o[:, col : col + width], in0=o[:, col : col + width], in1=s_of[(tn, col)][:, 0:width], op=ALU.add
                )

        def store(tn, c0, n):
            nc.sync.dma_start(out=outs[tn][:, c0 : c0 + n], in_=res[tn][:, c0 : c0 + n])

        def epilogue(ci):
            if ci < 3 or ci in (4, 5):
                sums(ci)
                cosines(ci, None)
                sines(ci, None)
                adds(ci)
            elif ci == 3:
                sums(3)
                inverse_rms(0)
                for lo in range(0, 3072, 1024):
                    scale_on_scalar(0, rs_of[0], lo, lo + 1024)
                cosines(3, None)
                sines(3, None)
                adds(3)
                scale_on_scalar(0, rs_of[0], 3072, DIM)
            elif ci == 6:
                sums(6)
                cosines(6, None)
            elif ci == 7:
                sums(7)
            else:
                sums(8)
                inverse_rms(1)
                scale_on_scalar(1, rs_of[1], 0, TILE_N)
                store(1, 0, TILE_N)
                sines(6, None)
                nc.vector.tensor_scalar(
                    out=res[1][:, TILE_N : 2 * TILE_N],
                    in0=res[1][:, TILE_N : 2 * TILE_N],
                    scalar1=rs_of[1][:],
                    scalar2=None,
                    op0=ALU.mult,
                )
                store(1, TILE_N, TILE_N)
                adds(6)
                for lo in range(1024, 3072, 1024):
                    scale_on_scalar(1, rs_of[1], lo, lo + 1024)
                    store(1, lo, 1024)
                for cj in (7, 8):
                    cosines(cj, rs_of[1])
                    sines(cj, rs_of[1])
                    adds(cj)
                    store(1, CHUNKS[cj][1], CHUNKS[cj][2])

        for i in range(len(pieces)):
            if i < len(TABLE_PLAN):
                for v, h in TABLE_PLAN[i]:
                    spread(v, h, tabs[v])
            run_passes(i)
            ci, g0, gp = pieces[i]
            if g0 + gp == GROUPS:
                epilogue(ci)
            for j in range(len(pieces)):
                if emit_after[j] == i:
                    load_piece(j)
                    for blk in STORE_AFTER.get(j, ()):
                        store(0, 1024 * blk, 1024)
